import numpy as np
import ml_dtypes


def mxq(x, axis, fmt="e4m3"):
    dtype, down = {"e4m3": (ml_dtypes.float8_e4m3fn, 7), "e5m2": (ml_dtypes.float8_e5m2, 14)}[fmt]
    v = np.moveaxis(np.asarray(x, np.float32).astype(ml_dtypes.bfloat16).astype(np.float64), axis, -1)
    blocks = v.reshape(v.shape[:-1] + (-1, 32))
    amax = np.abs(blocks).max(-1, keepdims=True)
    byte = np.maximum(np.where(amax > 0, np.frexp(amax)[1] - 1 + 127, 0) - down, 1)
    scale = np.exp2(byte - 127.0)
    codes = (blocks / scale).astype(np.float32).astype(dtype).astype(np.float64)
    return np.moveaxis((codes * scale).reshape(v.shape), -1, axis)


WIDE = False


def mx_kscale(k):
    if not WIDE:
        return np.ones(k)
    levels = np.array([20, -20, 10, -10, 0])
    a = np.random.permutation(np.resize(levels, k // 512 * 4)).reshape(k // 512, 4)
    idx = np.arange(k)
    return np.exp2(a[idx // 512, idx % 128 // 32])


BF16 = ml_dtypes.bfloat16


def bf(x):
    return np.asarray(x, np.float32).astype(BF16)


def f64(x):
    return np.asarray(x).astype(np.float64)


B, T, D, E, H, L = 128, 10, 1024, 128, 128, 2
TM = T - L
F = H + L * D + 1


def setup_inputs():
    u = mx_kscale(D)
    we = np.random.standard_normal((D, H)) / np.sqrt(H) / u[:, None]
    wy = np.random.standard_normal((D, L, D)) * 0.7 / np.sqrt(L * D) / u[:, None, None]
    wx = np.random.standard_normal((D, 1)) * 0.5 / u[:, None]
    x = np.random.standard_normal((B, T, D))
    emb = np.random.standard_normal((B, H)) * 0.5
    bg = np.random.standard_normal(D) * 0.3 / u
    g = np.random.standard_normal((B, TM, D)) * np.exp2(np.random.randint(-12, 1, (B, TM, 1))) * 4.0 * u
    return {"x": bf(x),
            "emb": bf(emb),
            "Wg": bf(np.concatenate([we, wy.reshape(D, L * D), wx], axis=1)),
            "bg": bf(bg),
            "grad_out": bf(g)}


def reference(x, emb, Wg, bg, grad_out):
    g = f64(grad_out)
    Wy = f64(Wg)[:, H:H + L * D].reshape(D, L, D)
    wx = f64(Wg)[:, -1]
    gq = mxq(g, 2, "e5m2")
    wq = mxq(Wy, 0, "e4m3")
    gx = np.zeros((B, T, D))
    for l in range(L):
        gx[:, l:TM + l, :] += (gq @ wq[:, l, :])
    gx[:, L:, :] += g * wx
    return gx

@@ -1,0 +1,207 @@
+from contextlib import ExitStack
+
+import concourse.mybir as mybir
+from concourse.masks import make_identity
+
+BF16 = mybir.dt.bfloat16
+F32 = mybir.dt.float32
+U32 = mybir.dt.uint32
+U8 = mybir.dt.uint8
+E4M3_X4 = mybir.dt.float8_e4m3fn_x4
+E5M2_X4 = mybir.dt.float8_e5m2_x4
+
+P = 128
+WINDOWS = 8
+STEPS = 10
+LATENTS = 1024
+LAGS = 2
+CONTEXT = 128
+PACK = 4
+K_PASS = P * PACK
+PASSES = LATENTS // K_PASS
+N_TILE = 512
+HALVES = LATENTS // N_TILE
+UNITS = HALVES * LAGS * PASSES
+WORDS = K_PASS // 2
+ADDS_FIRST = 2
+
+FLOPS = 2 * P * WINDOWS * LATENTS * LAGS * LATENTS
+BYTES = 2 * P * WINDOWS * LATENTS + 2 * LATENTS * (LAGS * LATENTS + 1) + 4 * P * STEPS * LATENTS
+
+
+def tile_npchangetransitionprior_pa_kernel(tc, x, emb, Wg, bg, grad_out, out):
+    nc = tc.nc
+    with ExitStack() as ctx:
+        keep = ctx.enter_context(tc.tile_pool(name="keep", bufs=1))
+        stage = ctx.enter_context(tc.tile_pool(name="stage", bufs=3))
+        banks = ctx.enter_context(tc.psum_pool(name="banks", bufs=8))
+        ctx.enter_context(tc.manual_schedule())
+
+        g_sb = keep.tile([P, WINDOWS * LATENTS], BF16)
+        g_rows = g_sb[:].rearrange("p (t d) -> p t d", t=WINDOWS)
+        g_words = g_sb[:].bitcast(F32).rearrange("p (t w) -> p t w", t=WINDOWS)
+        g_grouped = keep.tile([P, WINDOWS * PASSES * P * PACK], BF16, align_bytes=64)
+        g_grouped_words = g_grouped[:].bitcast(F32).rearrange(
+            "p (t c b u) -> p t c b u", t=WINDOWS, c=PASSES, b=P
+        )
+        g_codes = keep.tile([P, WINDOWS, PASSES, P], U32, align_bytes=64)
+        g_scales = keep.tile([P, WINDOWS, PASSES, P], U8, align_bytes=64)
+        w_raw = keep.tile([P, UNITS, PACK, N_TILE], BF16)
+        w_codes = keep.tile([P, UNITS, N_TILE], U32, align_bytes=64)
+        w_scales = keep.tile([P, UNITS, N_TILE], U8, align_bytes=64)
+        wx_col = keep.tile([P, LATENTS // P], BF16)
+        wx_rows = keep.tile([P, LATENTS], BF16)
+        res = keep.tile([P, STEPS, LATENTS], F32)
+        ident_f32 = keep.tile([P, P], F32)
+        ident_bf16 = keep.tile([P, P], BF16)
+        w_grouped = {}
+
+        def load_w(unit):
+            half, lag, c = unit // (LAGS * PASSES), (unit // PASSES) % LAGS, unit % PASSES
+            col0 = CONTEXT + lag * LATENTS + half * N_TILE
+            for u in range(2):
+                row0 = c * K_PASS + u * WORDS
+                nc.sync.dma_start(
+                    out=w_raw[:, unit, 2 * u : 2 * u + 2, :],
+                    in_=Wg[row0 : row0 + WORDS, col0 : col0 + N_TILE].rearrange(
+                        "(q e) n -> q e n", e=2
+                    ),
+                )
+
+        def load_g(pair):
+            nc.sync.dma_start(
+                out=g_rows[:, 2 * pair : 2 * pair + 2, :],
+                in_=grad_out[:, 2 * pair : 2 * pair + 2, :],
+            )
+
+        def regroup_w(unit, copy):
+            w_grouped[unit] = stage.tile([P, N_TILE, PACK], BF16, align_bytes=64, name="grouped")
+            copy(
+                out=w_grouped[unit][:].rearrange("p (n i) v -> p n v i", i=4),
+                in_=w_raw[:, unit].rearrange("p v (n i) -> p n v i", i=4),
+            )
+
+        def quantise_w(unit):
+            nc.vector.quantize_mx(
+                out=w_codes[:, unit, :].bitcast(E4M3_X4),
+                scales=w_scales[:, unit, :],
+                in_=w_grouped[unit][:].rearrange("p n v -> p (n v)"),
+            )
+
+        def transpose_g(t):
+            flipped = banks.tile([P, PASSES * 2, P], F32, tag="bank")
+            for cu in range(PASSES * 2):
+                nc.tensor.transpose(
+                    flipped[:, cu, :], g_words[:, t, cu * P : (cu + 1) * P], ident_f32[:]
+                )
+            nc.scalar.copy(
+                out=g_grouped_words[:, t],
+                in_=flipped[:].rearrange("p (c u) b -> p c b u", u=2),
+            )
+
+        def quantise_g(pair):
+            words = 2 * PASSES * P
+            nc.vector.quantize_mx(
+                out=g_codes[:, 2 * pair : 2 * pair + 2]
+                .rearrange("p t c b -> p (t c b)")
+                .bitcast(E5M2_X4),
+                scales=g_scales[:, 2 * pair : 2 * pair + 2].rearrange("p t c b -> p (t c b)"),
+                in_=g_grouped[:, pair * words * PACK : (pair + 1) * words * PACK],
+            )
+
+        def store(s, half):
+            cols = slice(half * N_TILE, (half + 1) * N_TILE)
+            nc.sync.dma_start(out=out[:, s, cols], in_=res[:, s, cols])
+
+        def own_latent_term(piece):
+            half, pair = piece // (WINDOWS // 2), piece % (WINDOWS // 2)
+            cols = slice(half * N_TILE, (half + 1) * N_TILE)
+            nc.vector.tensor_tensor(
+                out=res[:, 2 * pair + 2 : 2 * pair + 4, cols],
+                in0=g_rows[:, 2 * pair : 2 * pair + 2, cols],
+                in1=wx_rows[:, cols].unsqueeze(1).to_broadcast([P, 2, N_TILE]),
+                op=mybir.AluOpType.mult,
+            )
+            if 2 * pair + 3 == STEPS - 1:
+                store(STEPS - 1, half)
+
+        make_identity(nc, ident_f32[:])
+        nc.vector.tensor_copy(out=ident_bf16[:], in_=ident_f32[:])
+        with nc.allow_non_contiguous_dma(reason="wx is one column of Wg"):
+            nc.scalar.dma_start(
+                out=wx_col[:],
+                in_=Wg[:, CONTEXT + LAGS * LATENTS :].rearrange("(i p) o -> p (i o)", p=P),
+            )
+        load_w(0)
+        for pair in range(WINDOWS // 2):
+            load_g(pair)
+        for unit in range(1, UNITS):
+            load_w(unit)
+
+        for half in range(HALVES):
+            spread = banks.tile([P, N_TILE], F32, tag="bank")
+            for n in range(N_TILE // P):
+                i = half * (N_TILE // P) + n
+                nc.tensor.matmul(
+                    out=spread[:, n * P : (n + 1) * P],
+                    lhsT=wx_col[:, i : i + 1].to_broadcast([P, P]),
+                    rhs=ident_bf16[:],
+                    start=True,
+                    stop=True,
+                )
+            nc.vector.tensor_copy(
+                out=wx_rows[:, half * N_TILE : (half + 1) * N_TILE], in_=spread[:]
+            )
+
+        regroup_w(0, nc.scalar.copy)
+        for t in range(WINDOWS):
+            transpose_g(t)
+        own_latent_term(0)
+        quantise_w(0)
+        quantise_g(0)
+        own_latent_term(1)
+        quantise_g(1)
+        quantise_g(2)
+        regroup_w(1, nc.vector.tensor_copy)
+        quantise_g(3)
+        next_piece = 2
+
+        acc = {}
+        for unit in range(UNITS):
+            half, lag, c = unit // (LAGS * PASSES), (unit // PASSES) % LAGS, unit % PASSES
+            cols = slice(half * N_TILE, (half + 1) * N_TILE)
+            closing = lag == LAGS - 1 and c == PASSES - 1
+            if unit + 2 < UNITS:
+                regroup_w(unit + 2, nc.scalar.copy)
+            if not closing:
+                quantise_w(unit + 1)
+                own_latent_term(next_piece)
+                next_piece += 1
+            for t in range(WINDOWS):
+                if closing and t == ADDS_FIRST + 1 and unit + 1 < UNITS:
+                    quantise_w(unit + 1)
+                s = t + lag
+                first = c == 0 and (lag == 0 or s == WINDOWS)
+                last = c == PASSES - 1 and (lag == LAGS - 1 or s == 0)
+                if first:
+                    acc[s] = banks.tile([P, N_TILE], F32, tag="bank", name="acc")
+                nc.tensor.matmul_mx(
+                    out=acc[s][:],
+                    lhsT=g_codes[:, t, c, :].bitcast(E5M2_X4),
+                    lhsT_scale=g_scales[:, t, c, :],
+                    rhs=w_codes[:, unit, :].bitcast(E4M3_X4),
+                    rhs_scale=w_scales[:, unit, :],
+                    start=first,
+                    stop=last,
+                )
+                if last:
+                    if s < LAGS:
+                        nc.scalar.copy(out=res[:, s, cols], in_=acc[s][:])
+                    else:
+                        nc.vector.tensor_tensor(
+                            out=res[:, s, cols],
+                            in0=acc[s][:],
+                            in1=res[:, s, cols],
+                            op=mybir.AluOpType.add,
+                        )
+                    store(s, half)

@@ -113,8 +113,7 @@ def tile_npchangetransitionprior_pa_kernel(tc, x, emb, Wg, bg, grad_out, out):
             cols = slice(half * N_TILE, (half + 1) * N_TILE)
             nc.sync.dma_start(out=out[:, s, cols], in_=res[:, s, cols])
 
-        def own_latent_term(piece):
-            half, pair = piece // (WINDOWS // 2), piece % (WINDOWS // 2)
+        def own_latent_term(half, pair):
             cols = slice(half * N_TILE, (half + 1) * N_TILE)
             nc.vector.tensor_tensor(
                 out=res[:, 2 * pair + 2 : 2 * pair + 4, cols],
@@ -156,30 +155,25 @@ def tile_npchangetransitionprior_pa_kernel(tc, x, emb, Wg, bg, grad_out, out):
         regroup_w(0, nc.scalar.copy)
         for t in range(WINDOWS):
             transpose_g(t)
-        own_latent_term(0)
+        pairs = WINDOWS // 2
+        pieces = [(0, pair) for pair in range(pairs)]
+        pieces += [(1, (pair + pairs - 1) % pairs) for pair in range(pairs)]
+        own_latent_term(*pieces[0])
         quantise_w(0)
         quantise_g(0)
-        own_latent_term(1)
+        own_latent_term(*pieces[1])
         quantise_g(1)
         quantise_g(2)
         regroup_w(1, nc.vector.tensor_copy)
         quantise_g(3)
-        next_piece = 2
+        pieces_done = 2
 
         acc = {}
-        for unit in range(UNITS):
+
+        def passes(unit, windows):
             half, lag, c = unit // (LAGS * PASSES), (unit // PASSES) % LAGS, unit % PASSES
             cols = slice(half * N_TILE, (half + 1) * N_TILE)
-            closing = lag == LAGS - 1 and c == PASSES - 1
-            if unit + 2 < UNITS:
-                regroup_w(unit + 2, nc.scalar.copy)
-            if not closing:
-                quantise_w(unit + 1)
-                own_latent_term(next_piece)
-                next_piece += 1
-            for t in range(WINDOWS):
-                if closing and t == ADDS_FIRST + 1 and unit + 1 < UNITS:
-                    quantise_w(unit + 1)
+            for t in windows:
                 s = t + lag
                 first = c == 0 and (lag == 0 or s == WINDOWS)
                 last = c == PASSES - 1 and (lag == LAGS - 1 or s == 0)
@@ -205,3 +199,30 @@ def tile_npchangetransitionprior_pa_kernel(tc, x, emb, Wg, bg, grad_out, out):
                             op=mybir.AluOpType.add,
                         )
                     store(s, half)
+
+        for half in range(HALVES):
+            for c in range(PASSES):
+                unit = half * LAGS * PASSES + c
+                regroup_w(unit + 2, nc.scalar.copy)
+                quantise_w(unit + 1)
+                own_latent_term(*pieces[pieces_done])
+                pieces_done += 1
+                passes(unit, range(WINDOWS))
+            unit = half * LAGS * PASSES + PASSES
+            more = unit + 2 < UNITS
+            if more:
+                regroup_w(unit + 2, nc.scalar.copy)
+            quantise_w(unit + 1)
+            own_latent_term(*pieces[pieces_done])
+            pieces_done += 1
+            turn = WINDOWS // 2
+            passes(unit, range(0, turn))
+            passes(unit + 1, range(0, 1))
+            if more:
+                regroup_w(unit + 3, nc.scalar.copy)
+            passes(unit + 1, range(1, 1 + ADDS_FIRST))
+            if more:
+                quantise_w(unit + 2)
+            passes(unit + 1, range(1 + ADDS_FIRST, turn))
+            passes(unit, range(turn, WINDOWS))
+            passes(unit + 1, range(turn, WINDOWS))

@@ -54,6 +54,7 @@ def tile_npchangetransitionprior_pa_kernel(tc, x, emb, Wg, bg, grad_out, out):
         res = keep.tile([P, STEPS, LATENTS], F32)
         ident_f32 = keep.tile([P, P], F32)
         ident_bf16 = keep.tile([P, P], BF16)
+        table_warmer = keep.tile([P, 1], F32)
         w_grouped = {}
 
         def load_w(unit):
@@ -131,6 +132,7 @@ def tile_npchangetransitionprior_pa_kernel(tc, x, emb, Wg, bg, grad_out, out):
                 out=wx_col[:],
                 in_=Wg[:, CONTEXT + LAGS * LATENTS :].rearrange("(i p) o -> p (i o)", p=P),
             )
+        nc.scalar.copy(out=table_warmer[:], in_=ident_f32[:, 0:1])
         load_w(0)
         for pair in range(WINDOWS // 2):
             load_g(pair)

@@ -78,8 +78,8 @@ def tile_npchangetransitionprior_pa_kernel(tc, x, emb, Wg, bg, grad_out, out):
         def regroup_w(unit, copy):
             w_grouped[unit] = stage.tile([P, N_TILE, PACK], BF16, align_bytes=64, name="grouped")
             copy(
-                out=w_grouped[unit][:].rearrange("p (n i) v -> p n v i", i=4),
-                in_=w_raw[:, unit].rearrange("p v (n i) -> p n v i", i=4),
+                out=w_grouped[unit][:].rearrange("p (n i) v -> p n v i", i=8),
+                in_=w_raw[:, unit].rearrange("p v (n i) -> p n v i", i=8),
             )
 
         def quantise_w(unit):

from contextlib import ExitStack

import concourse.mybir as mybir
from concourse.masks import make_identity

BF16 = mybir.dt.bfloat16
F32 = mybir.dt.float32
U32 = mybir.dt.uint32
U8 = mybir.dt.uint8
E4M3_X4 = mybir.dt.float8_e4m3fn_x4
E5M2_X4 = mybir.dt.float8_e5m2_x4

P = 128
WINDOWS = 8
STEPS = 10
LATENTS = 1024
LAGS = 2
CONTEXT = 128
PACK = 4
K_PASS = P * PACK
PASSES = LATENTS // K_PASS
N_TILE = 512
HALVES = LATENTS // N_TILE
UNITS = HALVES * LAGS * PASSES
WORDS = K_PASS // 2
ADDS_FIRST = 2

FLOPS = 2 * P * WINDOWS * LATENTS * LAGS * LATENTS
BYTES = 2 * P * WINDOWS * LATENTS + 2 * LATENTS * (LAGS * LATENTS + 1) + 4 * P * STEPS * LATENTS


def tile_npchangetransitionprior_pa_kernel(tc, x, emb, Wg, bg, grad_out, out):
    nc = tc.nc
    with ExitStack() as ctx:
        keep = ctx.enter_context(tc.tile_pool(name="keep", bufs=1))
        stage = ctx.enter_context(tc.tile_pool(name="stage", bufs=3))
        banks = ctx.enter_context(tc.psum_pool(name="banks", bufs=8))
        ctx.enter_context(tc.manual_schedule())

        g_sb = keep.tile([P, WINDOWS * LATENTS], BF16)
        g_rows = g_sb[:].rearrange("p (t d) -> p t d", t=WINDOWS)
        g_words = g_sb[:].bitcast(F32).rearrange("p (t w) -> p t w", t=WINDOWS)
        g_grouped = keep.tile([P, WINDOWS * PASSES * P * PACK], BF16, align_bytes=64)
        g_grouped_words = g_grouped[:].bitcast(F32).rearrange(
            "p (t c b u) -> p t c b u", t=WINDOWS, c=PASSES, b=P
        )
        g_codes = keep.tile([P, WINDOWS, PASSES, P], U32, align_bytes=64)
        g_scales = keep.tile([P, WINDOWS, PASSES, P], U8, align_bytes=64)
        w_raw = keep.tile([P, UNITS, PACK, N_TILE], BF16)
        w_codes = keep.tile([P, UNITS, N_TILE], U32, align_bytes=64)
        w_scales = keep.tile([P, UNITS, N_TILE], U8, align_bytes=64)
        wx_col = keep.tile([P, LATENTS // P], BF16)
        wx_rows = keep.tile([P, LATENTS], BF16)
        res = keep.tile([P, STEPS, LATENTS], F32)
        ident_f32 = keep.tile([P, P], F32)
        ident_bf16 = keep.tile([P, P], BF16)
        table_warmer = keep.tile([P, 1], F32)
        w_grouped = {}

        def load_w(unit):
            half, lag, c = unit // (LAGS * PASSES), (unit // PASSES) % LAGS, unit % PASSES
            col0 = CONTEXT + lag * LATENTS + half * N_TILE
            for u in range(2):
                row0 = c * K_PASS + u * WORDS
                nc.sync.dma_start(
                    out=w_raw[:, unit, 2 * u : 2 * u + 2, :],
                    in_=Wg[row0 : row0 + WORDS, col0 : col0 + N_TILE].rearrange(
                        "(q e) n -> q e n", e=2
                    ),
                )

        def load_g(pair):
            nc.sync.dma_start(
                out=g_rows[:, 2 * pair : 2 * pair + 2, :],
                in_=grad_out[:, 2 * pair : 2 * pair + 2, :],
            )

        def regroup_w(unit, copy):
            w_grouped[unit] = stage.tile([P, N_TILE, PACK], BF16, align_bytes=64, name="grouped")
            copy(
                out=w_grouped[unit][:].rearrange("p (n i) v -> p n v i", i=8),
                in_=w_raw[:, unit].rearrange("p v (n i) -> p n v i", i=8),
            )

        def quantise_w(unit):
            nc.vector.quantize_mx(
                out=w_codes[:, unit, :].bitcast(E4M3_X4),
                scales=w_scales[:, unit, :],
                in_=w_grouped[unit][:].rearrange("p n v -> p (n v)"),
            )

        def transpose_g(t):
            flipped = banks.tile([P, PASSES * 2, P], F32, tag="bank")
            for cu in range(PASSES * 2):
                nc.tensor.transpose(
                    flipped[:, cu, :], g_words[:, t, cu * P : (cu + 1) * P], ident_f32[:]
                )
            nc.scalar.copy(
                out=g_grouped_words[:, t],
                in_=flipped[:].rearrange("p (c u) b -> p c b u", u=2),
            )

        def quantise_g(pair):
            words = 2 * PASSES * P
            nc.vector.quantize_mx(
                out=g_codes[:, 2 * pair : 2 * pair + 2]
                .rearrange("p t c b -> p (t c b)")
                .bitcast(E5M2_X4),
                scales=g_scales[:, 2 * pair : 2 * pair + 2].rearrange("p t c b -> p (t c b)"),
                in_=g_grouped[:, pair * words * PACK : (pair + 1) * words * PACK],
            )

        def store(s, half):
            cols = slice(half * N_TILE, (half + 1) * N_TILE)
            nc.sync.dma_start(out=out[:, s, cols], in_=res[:, s, cols])

        def own_latent_term(half, pair):
            cols = slice(half * N_TILE, (half + 1) * N_TILE)
            nc.vector.tensor_tensor(
                out=res[:, 2 * pair + 2 : 2 * pair + 4, cols],
                in0=g_rows[:, 2 * pair : 2 * pair + 2, cols],
                in1=wx_rows[:, cols].unsqueeze(1).to_broadcast([P, 2, N_TILE]),
                op=mybir.AluOpType.mult,
            )
            if 2 * pair + 3 == STEPS - 1:
                store(STEPS - 1, half)

        make_identity(nc, ident_f32[:])
        nc.vector.tensor_copy(out=ident_bf16[:], in_=ident_f32[:])
        with nc.allow_non_contiguous_dma(reason="wx is one column of Wg"):
            nc.scalar.dma_start(
                out=wx_col[:],
                in_=Wg[:, CONTEXT + LAGS * LATENTS :].rearrange("(i p) o -> p (i o)", p=P),
            )
        nc.scalar.copy(out=table_warmer[:], in_=ident_f32[:, 0:1])
        load_w(0)
        for pair in range(WINDOWS // 2):
            load_g(pair)
        for unit in range(1, UNITS):
            load_w(unit)

        for half in range(HALVES):
            spread = banks.tile([P, N_TILE], F32, tag="bank")
            for n in range(N_TILE // P):
                i = half * (N_TILE // P) + n
                nc.tensor.matmul(
                    out=spread[:, n * P : (n + 1) * P],
                    lhsT=wx_col[:, i : i + 1].to_broadcast([P, P]),
                    rhs=ident_bf16[:],
                    start=True,
                    stop=True,
                )
            nc.vector.tensor_copy(
                out=wx_rows[:, half * N_TILE : (half + 1) * N_TILE], in_=spread[:]
            )

        regroup_w(0, nc.scalar.copy)
        for t in range(WINDOWS):
            transpose_g(t)
        pairs = WINDOWS // 2
        pieces = [(0, pair) for pair in range(pairs)]
        pieces += [(1, (pair + pairs - 1) % pairs) for pair in range(pairs)]
        own_latent_term(*pieces[0])
        quantise_w(0)
        quantise_g(0)
        own_latent_term(*pieces[1])
        quantise_g(1)
        quantise_g(2)
        regroup_w(1, nc.vector.tensor_copy)
        quantise_g(3)
        pieces_done = 2

        acc = {}

        def passes(unit, windows):
            half, lag, c = unit // (LAGS * PASSES), (unit // PASSES) % LAGS, unit % PASSES
            cols = slice(half * N_TILE, (half + 1) * N_TILE)
            for t in windows:
                s = t + lag
                first = c == 0 and (lag == 0 or s == WINDOWS)
                last = c == PASSES - 1 and (lag == LAGS - 1 or s == 0)
                if first:
                    acc[s] = banks.tile([P, N_TILE], F32, tag="bank", name="acc")
                nc.tensor.matmul_mx(
                    out=acc[s][:],
                    lhsT=g_codes[:, t, c, :].bitcast(E5M2_X4),
                    lhsT_scale=g_scales[:, t, c, :],
                    rhs=w_codes[:, unit, :].bitcast(E4M3_X4),
                    rhs_scale=w_scales[:, unit, :],
                    start=first,
                    stop=last,
                )
                if last:
                    if s < LAGS:
                        nc.scalar.copy(out=res[:, s, cols], in_=acc[s][:])
                    else:
                        nc.vector.tensor_tensor(
                            out=res[:, s, cols],
                            in0=acc[s][:],
                            in1=res[:, s, cols],
                            op=mybir.AluOpType.add,
                        )
                    store(s, half)

        for half in range(HALVES):
            for c in range(PASSES):
                unit = half * LAGS * PASSES + c
                regroup_w(unit + 2, nc.scalar.copy)
                quantise_w(unit + 1)
                own_latent_term(*pieces[pieces_done])
                pieces_done += 1
                passes(unit, range(WINDOWS))
            unit = half * LAGS * PASSES + PASSES
            more = unit + 2 < UNITS
            if more:
                regroup_w(unit + 2, nc.scalar.copy)
            quantise_w(unit + 1)
            own_latent_term(*pieces[pieces_done])
            pieces_done += 1
            turn = WINDOWS // 2
            passes(unit, range(0, turn))
            passes(unit + 1, range(0, 1))
            if more:
                regroup_w(unit + 3, nc.scalar.copy)
            passes(unit + 1, range(1, 1 + ADDS_FIRST))
            if more:
                quantise_w(unit + 2)
            passes(unit + 1, range(1 + ADDS_FIRST, turn))
            passes(unit, range(turn, WINDOWS))
            passes(unit + 1, range(turn, WINDOWS))
